import numpy as np
import ml_dtypes


def mxq(x, axis, fmt="e4m3"):
    dtype, down = {"e4m3": (ml_dtypes.float8_e4m3fn, 7), "e5m2": (ml_dtypes.float8_e5m2, 14)}[fmt]
    v = np.moveaxis(np.asarray(x, np.float32).astype(ml_dtypes.bfloat16).astype(np.float64), axis, -1)
    blocks = v.reshape(v.shape[:-1] + (-1, 32))
    amax = np.abs(blocks).max(-1, keepdims=True)
    byte = np.maximum(np.where(amax > 0, np.frexp(amax)[1] - 1 + 127, 0) - down, 1)
    scale = np.exp2(byte - 127.0)
    codes = (blocks / scale).astype(np.float32).astype(dtype).astype(np.float64)
    return np.moveaxis((codes * scale).reshape(v.shape), -1, axis)


WIDE = False


def mx_kscale(k):
    if not WIDE:
        return np.ones(k)
    levels = np.array([10, -10, 5, -5, 0])
    if k % 512:
        return np.exp2(np.random.permutation(np.resize(levels, k // 32))).repeat(32)
    a = np.empty((k // 512, 16))
    for p in range(k // 512):
        a[p, :8] = np.random.permutation(np.resize(levels, 8))
        for g in range(8):
            far = levels[np.abs(levels - a[p, g]) >= 10]
            a[p, g + 8] = far[np.random.randint(len(far))]
    return np.exp2(a.ravel()).repeat(32)


BF16 = ml_dtypes.bfloat16


def bf(x):
    return np.asarray(x, np.float32).astype(BF16)


def f64(x):
    return np.asarray(x).astype(np.float64)


N, P, D, E, F = 5120, 3, 512, 512, 128
BN_EPS = 1e-5


def setup_inputs():
    t = mx_kscale(E)
    h = 1.2 * np.random.standard_normal((N, P, E)) + 0.6 * np.random.standard_normal((1, P, E))
    return {"h_sage": bf(h * t),
            "w1b": bf(np.random.standard_normal((E, F)) / np.sqrt(E) / t[:, None]),
            "w2b": bf(np.random.standard_normal((E, F)) / np.sqrt(E) / t[:, None]),
            "gamma": bf(1.0 + 0.2 * np.random.standard_normal(F)),
            "beta": bf(0.3 * np.random.standard_normal(F))}


def reference(h_sage, w1b, w2b, gamma, beta):
    h = f64(h_sage)
    neigh = (h.sum(axis=1, keepdims=True) - h) * 0.5
    out = (mxq(h[:, 0, :], 1, "e4m3") @ mxq(f64(w2b), 0, "e4m3")) + (mxq(neigh[:, 0, :], 1, "e4m3") @ mxq(f64(w1b), 0, "e4m3"))
    mean = out.mean(axis=0)
    var = out.var(axis=0)
    out = (out - mean) / np.sqrt(var + BN_EPS) * f64(gamma) + f64(beta)
    return 1.0 / (1.0 + np.exp(-out))

@@ -1,0 +1,241 @@
+from contextlib import ExitStack
+
+import concourse.mybir as mybir
+from concourse.masks import make_identity
+
+BF16 = mybir.dt.bfloat16
+F32 = mybir.dt.float32
+U32 = mybir.dt.uint32
+U8 = mybir.dt.uint8
+FP8X4 = mybir.dt.float8_e4m3fn_x4
+ALU = mybir.AluOpType
+ACT = mybir.ActivationFunctionType
+
+P = 128
+PACK = 4
+HALVES = 2
+ITEMS = 5120
+HOPS = 3
+FEATS = 512
+COLS = 128
+BN_EPS = 1e-5
+BN_STATS_DIM = 6
+
+TILES = ITEMS // P
+BANK_TILES = 2
+PIECES = (1, 1, 2) + (4,) * 9
+Y_KEPT = 4
+assert sum(PIECES) == TILES
+
+FLOPS = 2 * 2 * ITEMS * FEATS * COLS
+
+
+def tile_dogtaitujuanji_pb_t_kernel(tc, h_sage, w1b, w2b, gamma, beta, out):
+    nc = tc.nc
+    h_rows = h_sage.rearrange("(p j) q k -> p j q k", j=TILES)
+    out_rows = out.rearrange("(p j) f -> p j f", j=TILES)
+    n_pieces = len(PIECES)
+    first_tile = [sum(PIECES[:i]) for i in range(n_pieces)]
+
+    with ExitStack() as ctx:
+        ctx.enter_context(tc.manual_schedule())
+        const = ctx.enter_context(tc.tile_pool(name="const", bufs=1))
+        h_pool = ctx.enter_context(tc.tile_pool(name="h", bufs=1))
+        y_pool = ctx.enter_context(tc.tile_pool(name="y_sbuf", bufs=1))
+        grouped = ctx.enter_context(tc.tile_pool(name="grouped", bufs=3))
+        packed = ctx.enter_context(tc.tile_pool(name="packed", bufs=3))
+        result = ctx.enter_context(tc.tile_pool(name="result", bufs=3))
+        rows_pool = ctx.enter_context(tc.tile_pool(name="rows", bufs=1))
+        psum_turn = ctx.enter_context(tc.psum_pool(name="psum_turn", bufs=4))
+        psum_y = ctx.enter_context(tc.psum_pool(name="psum_y", bufs=Y_KEPT))
+
+        h_pieces = []
+        for i, n_tiles in enumerate(PIECES):
+            h_piece = h_pool.tile([P, n_tiles, HOPS, FEATS], BF16, name="h_piece%d" % i)
+            nc.sync.dma_start(
+                out=h_piece[:], in_=h_rows[:, first_tile[i] : first_tile[i] + n_tiles]
+            )
+            h_pieces.append(h_piece)
+
+        w_raw = const.tile([P, 2, PACK, COLS], BF16)
+        nc.scalar.dma_start(out=w_raw[:, 0], in_=w2b.rearrange("(p t) f -> p t f", t=PACK))
+        nc.scalar.dma_start(out=w_raw[:, 1], in_=w1b.rearrange("(p t) f -> p t f", t=PACK))
+        gamma_bf = const.tile([P, 1], BF16)
+        beta_bf = const.tile([P, 1], BF16)
+        nc.scalar.dma_start(out=gamma_bf[:], in_=gamma.rearrange("(f o) -> f o", o=1))
+        nc.scalar.dma_start(out=beta_bf[:], in_=beta.rearrange("(f o) -> f o", o=1))
+
+        ident_f32 = const.tile([P, P], F32)
+        make_identity(nc, ident_f32[:])
+        ident_bf16 = const.tile([P, P], BF16)
+        make_identity(nc, ident_bf16[:])
+        minus_half = const.tile([P, 1], F32)
+        nc.vector.memset(minus_half[:], -0.5)
+        warm = const.tile([P, 1], F32)
+        nc.vector.memset(warm[:], 0.0)
+        nc.scalar.activation(out=warm[:], in_=warm[:], func=ACT.Sigmoid)
+
+        w_grouped = const.tile([P, 2, COLS, PACK], BF16, align_bytes=64)
+        nc.vector.tensor_copy(out=w_grouped[:], in_=w_raw[:].rearrange("p i t f -> p i f t"))
+        w_codes = const.tile([P, 2 * COLS], U32, align_bytes=64)
+        w_scales = const.tile([P, 2 * COLS], U8, align_bytes=64)
+        nc.vector.quantize_mx(
+            out=w_codes[:].bitcast(FP8X4),
+            scales=w_scales[:],
+            in_=w_grouped[:].rearrange("p i f t -> p (i f t)"),
+        )
+
+        stats = const.tile([P, n_pieces, BN_STATS_DIM], F32)
+
+        def banks_of(n_tiles):
+            return [(first, min(BANK_TILES, n_tiles - first)) for first in range(0, n_tiles, BANK_TILES)]
+
+        def add_hops(i):
+            h_piece = h_pieces[i]
+            n_tiles = PIECES[i]
+            sum_rows = grouped.tile([P, n_tiles, FEATS], BF16, tag="sum_rows")
+            for first, count in banks_of(n_tiles):
+                tiles = slice(first, first + count)
+                nc.vector.tensor_tensor(
+                    out=sum_rows[:, tiles, :],
+                    in0=h_piece[:, tiles, 1, :],
+                    in1=h_piece[:, tiles, 2, :],
+                    op=ALU.add,
+                )
+            return sum_rows
+
+        def turn_self(i):
+            h_piece = h_pieces[i]
+            n_tiles = PIECES[i]
+            self_t = grouped.tile([P, n_tiles * P * PACK], BF16, tag="self_t", align_bytes=64)
+            for first, count in banks_of(n_tiles):
+                bank = psum_turn.tile([P, HALVES * count * P], F32, tag="turn")
+                for g in range(count):
+                    words = h_piece[:, first + g, 0, :].bitcast(F32)
+                    for u in range(HALVES):
+                        at = (u * count + g) * P
+                        nc.tensor.transpose(
+                            bank[:, at : at + P], words[:, u :: HALVES], ident_f32[:]
+                        )
+                nc.scalar.copy(
+                    out=self_t[:]
+                    .bitcast(F32)
+                    .rearrange("p (c u) -> p c u", u=HALVES)[:, first * P : (first + count) * P, :],
+                    in_=bank[:].rearrange("p (u c) -> p c u", u=HALVES),
+                )
+            return self_t
+
+        def turn_neigh(i, sum_rows):
+            n_tiles = PIECES[i]
+            neigh_t = grouped.tile([P, n_tiles * P * PACK], BF16, tag="neigh_t", align_bytes=64)
+            for first, count in banks_of(n_tiles):
+                bank = psum_turn.tile([P, count * PACK * P], BF16, tag="turn")
+                for g in range(count):
+                    for t in range(PACK):
+                        at = (g * PACK + t) * P
+                        nc.tensor.transpose(
+                            bank[:, at : at + P],
+                            sum_rows[:, first + g, t::PACK],
+                            ident_bf16[:],
+                        )
+                nc.scalar.mul(
+                    out=neigh_t[:].rearrange("p (g c t) -> p g c t", c=P, t=PACK)[
+                        :, first : first + count
+                    ],
+                    in_=bank[:].rearrange("p (g t c) -> p g c t", g=count, t=PACK),
+                    mul=0.5,
+                )
+            return neigh_t
+
+        def quantise_piece(i, values):
+            width = PIECES[i] * P
+            operands = []
+            for name, tile_bf16 in zip(("self", "neigh"), values):
+                words = packed.tile([P, width], U32, tag=name + "_codes", align_bytes=64)
+                scales = packed.tile([P, width], U8, tag=name + "_scales", align_bytes=64)
+                nc.vector.quantize_mx(
+                    out=words[:].bitcast(FP8X4), scales=scales[:], in_=tile_bf16[:]
+                )
+                operands.append((words, scales))
+            return operands
+
+        def multiply_piece(operands, y_psum):
+            for w_index, (words, scales) in enumerate(operands):
+                w_cols = slice(w_index * COLS, (w_index + 1) * COLS)
+                nc.tensor.matmul_mx(
+                    out=y_psum[:],
+                    lhsT=w_codes[:, w_cols].bitcast(FP8X4),
+                    lhsT_scale=w_scales[:, w_cols],
+                    rhs=words[:].bitcast(FP8X4),
+                    rhs_scale=scales[:],
+                    start=(w_index == 0),
+                    stop=(w_index == 1),
+                )
+
+        def measure_piece(i, y_psum):
+            nc.vector.bn_stats(out=stats[:, i, :], in_=y_psum[:])
+            if i >= n_pieces - Y_KEPT:
+                return y_psum
+            y_sbuf = y_pool.tile([P, PIECES[i] * P], F32, name="y_sbuf%d" % i)
+            nc.vector.tensor_copy(out=y_sbuf[:], in_=y_psum[:])
+            return y_sbuf
+
+        turned = {}
+        products = {}
+        y_pieces = []
+        for step in range(n_pieces + 2):
+            turning = step < n_pieces
+            multiplying = 1 <= step <= n_pieces
+            if turning:
+                sum_rows = add_hops(step)
+                turned[step] = (turn_self(step), turn_neigh(step, sum_rows))
+            if multiplying:
+                y_psum = psum_y.tile([P, PIECES[step - 1] * P], F32, tag="y")
+                products[step - 1] = y_psum
+                multiply_piece(quantise_piece(step - 1, turned[step - 1]), y_psum)
+            if step >= 2:
+                y_pieces.append(measure_piece(step - 2, products[step - 2]))
+
+        gamma_f = const.tile([P, 1], F32)
+        neg_gamma_f = const.tile([P, 1], F32)
+        beta_f = const.tile([P, 1], F32)
+        mean_var = const.tile([P, 2], F32)
+        var_eps = const.tile([P, 1], F32)
+        neg_gamma_mean = const.tile([P, 1], F32)
+        rstd = const.tile([P, 1], F32)
+        gain = const.tile([P, 1], F32)
+        shift = const.tile([P, 1], F32)
+        nc.vector.bn_aggr(out=mean_var[:], in_=stats[:].rearrange("p i s -> p (i s)"))
+        nc.vector.tensor_scalar_add(out=var_eps[:], in0=mean_var[:, 1:2], scalar1=BN_EPS)
+        nc.gpsimd.tensor_tensor(out=rstd[:], in0=var_eps[:], in1=minus_half[:], op=ALU.pow)
+        nc.vector.tensor_copy(out=gamma_f[:], in_=gamma_bf[:])
+        nc.vector.tensor_copy(out=beta_f[:], in_=beta_bf[:])
+        nc.vector.tensor_scalar_mul(out=neg_gamma_f[:], in0=gamma_bf[:], scalar1=-1.0)
+        nc.vector.tensor_mul(out=neg_gamma_mean[:], in0=mean_var[:, 0:1], in1=neg_gamma_f[:])
+        nc.vector.tensor_mul(out=gain[:], in0=gamma_f[:], in1=rstd[:])
+        nc.vector.tensor_scalar(
+            out=shift[:],
+            in0=neg_gamma_mean[:],
+            scalar1=rstd[:, 0:1],
+            scalar2=beta_f[:, 0:1],
+            op0=ALU.mult,
+            op1=ALU.add,
+        )
+
+        for i, n_tiles in enumerate(PIECES):
+            sig = result.tile([P, n_tiles * P], F32, tag="sig")
+            nc.scalar.activation(
+                out=sig[:],
+                in_=y_pieces[i][:],
+                func=ACT.Sigmoid,
+                bias=shift[:, 0:1],
+                scale=gain[:, 0:1],
+            )
+            back = psum_turn.tile([P, n_tiles, COLS], F32, tag="turn")
+            for g in range(n_tiles):
+                nc.tensor.transpose(back[:, g, :], sig[:, g * P : (g + 1) * P], ident_f32[:])
+            rows = rows_pool.tile([P, n_tiles, COLS], F32, name="rows%d" % i)
+            nc.vector.tensor_copy(out=rows[:], in_=back[:])
+            nc.sync.dma_start(
+                out=out_rows[:, first_tile[i] : first_tile[i] + n_tiles, :], in_=rows[:]
+            )

@@ -14,6 +14,7 @@ ACT = mybir.ActivationFunctionType
 P = 128
 PACK = 4
 HALVES = 2
+PAIR = 2
 ITEMS = 5120
 HOPS = 3
 FEATS = 512
@@ -67,8 +68,6 @@ def tile_dogtaitujuanji_pb_t_kernel(tc, h_sage, w1b, w2b, gamma, beta, out):
 
         ident_f32 = const.tile([P, P], F32)
         make_identity(nc, ident_f32[:])
-        ident_bf16 = const.tile([P, P], BF16)
-        make_identity(nc, ident_bf16[:])
         minus_half = const.tile([P, 1], F32)
         nc.vector.memset(minus_half[:], -0.5)
         warm = const.tile([P, 1], F32)
@@ -76,7 +75,10 @@ def tile_dogtaitujuanji_pb_t_kernel(tc, h_sage, w1b, w2b, gamma, beta, out):
         nc.scalar.activation(out=warm[:], in_=warm[:], func=ACT.Sigmoid)
 
         w_grouped = const.tile([P, 2, COLS, PACK], BF16, align_bytes=64)
-        nc.vector.tensor_copy(out=w_grouped[:], in_=w_raw[:].rearrange("p i t f -> p i f t"))
+        nc.vector.tensor_copy(out=w_grouped[:, 0], in_=w_raw[:, 0].rearrange("p t f -> p f t"))
+        nc.vector.tensor_scalar_mul(
+            out=w_grouped[:, 1], in0=w_raw[:, 1].rearrange("p t f -> p f t"), scalar1=0.5
+        )
         w_codes = const.tile([P, 2 * COLS], U32, align_bytes=64)
         w_scales = const.tile([P, 2 * COLS], U8, align_bytes=64)
         nc.vector.quantize_mx(
@@ -93,59 +95,38 @@ def tile_dogtaitujuanji_pb_t_kernel(tc, h_sage, w1b, w2b, gamma, beta, out):
         def add_hops(i):
             h_piece = h_pieces[i]
             n_tiles = PIECES[i]
-            sum_rows = grouped.tile([P, n_tiles, FEATS], BF16, tag="sum_rows")
+            sum_rows = grouped.tile([P, HALVES, n_tiles, FEATS // HALVES], BF16, tag="sum_rows")
             for first, count in banks_of(n_tiles):
                 tiles = slice(first, first + count)
                 nc.vector.tensor_tensor(
-                    out=sum_rows[:, tiles, :],
-                    in0=h_piece[:, tiles, 1, :],
-                    in1=h_piece[:, tiles, 2, :],
+                    out=sum_rows[:, :, tiles, :].rearrange("p u g (w e) -> p g w u e", e=PAIR),
+                    in0=h_piece[:, tiles, 1, :].rearrange("p g (w u e) -> p g w u e", u=HALVES, e=PAIR),
+                    in1=h_piece[:, tiles, 2, :].rearrange("p g (w u e) -> p g w u e", u=HALVES, e=PAIR),
                     op=ALU.add,
                 )
             return sum_rows
 
-        def turn_self(i):
-            h_piece = h_pieces[i]
-            n_tiles = PIECES[i]
-            self_t = grouped.tile([P, n_tiles * P * PACK], BF16, tag="self_t", align_bytes=64)
+        def turn(tag, n_tiles, words_of):
+            turned_t = grouped.tile([P, n_tiles * P * PACK], BF16, tag=tag, align_bytes=64)
             for first, count in banks_of(n_tiles):
                 bank = psum_turn.tile([P, HALVES * count * P], F32, tag="turn")
                 for g in range(count):
-                    words = h_piece[:, first + g, 0, :].bitcast(F32)
                     for u in range(HALVES):
                         at = (u * count + g) * P
-                        nc.tensor.transpose(
-                            bank[:, at : at + P], words[:, u :: HALVES], ident_f32[:]
-                        )
+                        nc.tensor.transpose(bank[:, at : at + P], words_of(first + g, u), ident_f32[:])
                 nc.scalar.copy(
-                    out=self_t[:]
+                    out=turned_t[:]
                     .bitcast(F32)
                     .rearrange("p (c u) -> p c u", u=HALVES)[:, first * P : (first + count) * P, :],
                     in_=bank[:].rearrange("p (u c) -> p c u", u=HALVES),
                 )
-            return self_t
+            return turned_t
+
+        def turn_self(i):
+            return turn("self_t", PIECES[i], lambda g, u: h_pieces[i][:, g, 0, :].bitcast(F32)[:, u::HALVES])
 
         def turn_neigh(i, sum_rows):
-            n_tiles = PIECES[i]
-            neigh_t = grouped.tile([P, n_tiles * P * PACK], BF16, tag="neigh_t", align_bytes=64)
-            for first, count in banks_of(n_tiles):
-                bank = psum_turn.tile([P, count * PACK * P], BF16, tag="turn")
-                for g in range(count):
-                    for t in range(PACK):
-                        at = (g * PACK + t) * P
-                        nc.tensor.transpose(
-                            bank[:, at : at + P],
-                            sum_rows[:, first + g, t::PACK],
-                            ident_bf16[:],
-                        )
-                nc.scalar.mul(
-                    out=neigh_t[:].rearrange("p (g c t) -> p g c t", c=P, t=PACK)[
-                        :, first : first + count
-                    ],
-                    in_=bank[:].rearrange("p (g t c) -> p g c t", g=count, t=PACK),
-                    mul=0.5,
-                )
-            return neigh_t
+            return turn("neigh_t", PIECES[i], lambda g, u: sum_rows[:, u, g, :].bitcast(F32))
 
         def quantise_piece(i, values):
             width = PIECES[i] * P
@@ -177,7 +158,7 @@ def tile_dogtaitujuanji_pb_t_kernel(tc, h_sage, w1b, w2b, gamma, beta, out):
             if i >= n_pieces - Y_KEPT:
                 return y_psum
             y_sbuf = y_pool.tile([P, PIECES[i] * P], F32, name="y_sbuf%d" % i)
-            nc.vector.tensor_copy(out=y_sbuf[:], in_=y_psum[:])
+            nc.scalar.copy(out=y_sbuf[:], in_=y_psum[:])
             return y_sbuf
 
         turned = {}

@@ -15,6 +15,7 @@ P = 128
 PACK = 4
 HALVES = 2
 PAIR = 2
+SIDES = 2
 ITEMS = 5120
 HOPS = 3
 FEATS = 512
@@ -23,42 +24,50 @@ BN_EPS = 1e-5
 BN_STATS_DIM = 6
 
 TILES = ITEMS // P
-BANK_TILES = 2
-PIECES = (1, 1, 2) + (4,) * 9
+UNITS = (1, 1) + (2,) * 18 + (1, 1)
+MULTIPLY_LAG = 2
+MEASURE_LAG = 3
+WEIGHTS_STEP = 1
+AFFINE_STEP = 4
+Y_TILES = 4
+Y_BANKS = TILES // Y_TILES
 Y_KEPT = 4
-assert sum(PIECES) == TILES
+CHUNKS = (1, 1, 2) + (4,) * 8 + (2, 1, 1)
+assert sum(UNITS) == sum(CHUNKS) == TILES
 
 FLOPS = 2 * 2 * ITEMS * FEATS * COLS
+
+
+def starts_of(sizes):
+    return [sum(sizes[:i]) for i in range(len(sizes))]
 
 
 def tile_dogtaitujuanji_pb_t_kernel(tc, h_sage, w1b, w2b, gamma, beta, out):
     nc = tc.nc
     h_rows = h_sage.rearrange("(p j) q k -> p j q k", j=TILES)
     out_rows = out.rearrange("(p j) f -> p j f", j=TILES)
-    n_pieces = len(PIECES)
-    first_tile = [sum(PIECES[:i]) for i in range(n_pieces)]
+    n_units = len(UNITS)
+    unit_start = starts_of(UNITS)
 
     with ExitStack() as ctx:
         ctx.enter_context(tc.manual_schedule())
         const = ctx.enter_context(tc.tile_pool(name="const", bufs=1))
         h_pool = ctx.enter_context(tc.tile_pool(name="h", bufs=1))
         y_pool = ctx.enter_context(tc.tile_pool(name="y_sbuf", bufs=1))
-        grouped = ctx.enter_context(tc.tile_pool(name="grouped", bufs=3))
-        packed = ctx.enter_context(tc.tile_pool(name="packed", bufs=3))
+        grouped = ctx.enter_context(tc.tile_pool(name="grouped", bufs=4))
+        packed = ctx.enter_context(tc.tile_pool(name="packed", bufs=4))
         result = ctx.enter_context(tc.tile_pool(name="result", bufs=3))
         rows_pool = ctx.enter_context(tc.tile_pool(name="rows", bufs=1))
         psum_turn = ctx.enter_context(tc.psum_pool(name="psum_turn", bufs=4))
         psum_y = ctx.enter_context(tc.psum_pool(name="psum_y", bufs=Y_KEPT))
 
-        h_pieces = []
-        for i, n_tiles in enumerate(PIECES):
-            h_piece = h_pool.tile([P, n_tiles, HOPS, FEATS], BF16, name="h_piece%d" % i)
-            nc.sync.dma_start(
-                out=h_piece[:], in_=h_rows[:, first_tile[i] : first_tile[i] + n_tiles]
-            )
-            h_pieces.append(h_piece)
+        h_units = []
+        for i, (start, n_tiles) in enumerate(zip(unit_start, UNITS)):
+            h_unit = h_pool.tile([P, n_tiles, HOPS, FEATS], BF16, name="h_unit%d" % i)
+            nc.sync.dma_start(out=h_unit[:], in_=h_rows[:, start : start + n_tiles])
+            h_units.append(h_unit)
 
-        w_raw = const.tile([P, 2, PACK, COLS], BF16)
+        w_raw = const.tile([P, SIDES, PACK, COLS], BF16)
         nc.scalar.dma_start(out=w_raw[:, 0], in_=w2b.rearrange("(p t) f -> p t f", t=PACK))
         nc.scalar.dma_start(out=w_raw[:, 1], in_=w1b.rearrange("(p t) f -> p t f", t=PACK))
         gamma_bf = const.tile([P, 1], BF16)
@@ -74,112 +83,128 @@ def tile_dogtaitujuanji_pb_t_kernel(tc, h_sage, w1b, w2b, gamma, beta, out):
         nc.vector.memset(warm[:], 0.0)
         nc.scalar.activation(out=warm[:], in_=warm[:], func=ACT.Sigmoid)
 
-        w_grouped = const.tile([P, 2, COLS, PACK], BF16, align_bytes=64)
-        nc.vector.tensor_copy(out=w_grouped[:, 0], in_=w_raw[:, 0].rearrange("p t f -> p f t"))
-        nc.vector.tensor_scalar_mul(
-            out=w_grouped[:, 1], in0=w_raw[:, 1].rearrange("p t f -> p f t"), scalar1=0.5
-        )
-        w_codes = const.tile([P, 2 * COLS], U32, align_bytes=64)
-        w_scales = const.tile([P, 2 * COLS], U8, align_bytes=64)
-        nc.vector.quantize_mx(
-            out=w_codes[:].bitcast(FP8X4),
-            scales=w_scales[:],
-            in_=w_grouped[:].rearrange("p i f t -> p (i f t)"),
-        )
+        w_grouped = const.tile([P, SIDES, COLS, PACK], BF16, align_bytes=64)
+        w_codes = const.tile([P, SIDES * COLS], U32, align_bytes=64)
+        w_scales = const.tile([P, SIDES * COLS], U8, align_bytes=64)
 
-        stats = const.tile([P, n_pieces, BN_STATS_DIM], F32)
-
-        def banks_of(n_tiles):
-            return [(first, min(BANK_TILES, n_tiles - first)) for first in range(0, n_tiles, BANK_TILES)]
-
-        def add_hops(i):
-            h_piece = h_pieces[i]
-            n_tiles = PIECES[i]
-            sum_rows = grouped.tile([P, HALVES, n_tiles, FEATS // HALVES], BF16, tag="sum_rows")
-            for first, count in banks_of(n_tiles):
-                tiles = slice(first, first + count)
-                nc.vector.tensor_tensor(
-                    out=sum_rows[:, :, tiles, :].rearrange("p u g (w e) -> p g w u e", e=PAIR),
-                    in0=h_piece[:, tiles, 1, :].rearrange("p g (w u e) -> p g w u e", u=HALVES, e=PAIR),
-                    in1=h_piece[:, tiles, 2, :].rearrange("p g (w u e) -> p g w u e", u=HALVES, e=PAIR),
-                    op=ALU.add,
-                )
-            return sum_rows
-
-        def turn(tag, n_tiles, words_of):
-            turned_t = grouped.tile([P, n_tiles * P * PACK], BF16, tag=tag, align_bytes=64)
-            for first, count in banks_of(n_tiles):
-                bank = psum_turn.tile([P, HALVES * count * P], F32, tag="turn")
-                for g in range(count):
-                    for u in range(HALVES):
-                        at = (u * count + g) * P
-                        nc.tensor.transpose(bank[:, at : at + P], words_of(first + g, u), ident_f32[:])
-                nc.scalar.copy(
-                    out=turned_t[:]
-                    .bitcast(F32)
-                    .rearrange("p (c u) -> p c u", u=HALVES)[:, first * P : (first + count) * P, :],
-                    in_=bank[:].rearrange("p (u c) -> p c u", u=HALVES),
-                )
-            return turned_t
-
-        def turn_self(i):
-            return turn("self_t", PIECES[i], lambda g, u: h_pieces[i][:, g, 0, :].bitcast(F32)[:, u::HALVES])
-
-        def turn_neigh(i, sum_rows):
-            return turn("neigh_t", PIECES[i], lambda g, u: sum_rows[:, u, g, :].bitcast(F32))
-
-        def quantise_piece(i, values):
-            width = PIECES[i] * P
-            operands = []
-            for name, tile_bf16 in zip(("self", "neigh"), values):
-                words = packed.tile([P, width], U32, tag=name + "_codes", align_bytes=64)
-                scales = packed.tile([P, width], U8, tag=name + "_scales", align_bytes=64)
-                nc.vector.quantize_mx(
-                    out=words[:].bitcast(FP8X4), scales=scales[:], in_=tile_bf16[:]
-                )
-                operands.append((words, scales))
-            return operands
-
-        def multiply_piece(operands, y_psum):
-            for w_index, (words, scales) in enumerate(operands):
-                w_cols = slice(w_index * COLS, (w_index + 1) * COLS)
-                nc.tensor.matmul_mx(
-                    out=y_psum[:],
-                    lhsT=w_codes[:, w_cols].bitcast(FP8X4),
-                    lhsT_scale=w_scales[:, w_cols],
-                    rhs=words[:].bitcast(FP8X4),
-                    rhs_scale=scales[:],
-                    start=(w_index == 0),
-                    stop=(w_index == 1),
-                )
-
-        def measure_piece(i, y_psum):
-            nc.vector.bn_stats(out=stats[:, i, :], in_=y_psum[:])
-            if i >= n_pieces - Y_KEPT:
-                return y_psum
-            y_sbuf = y_pool.tile([P, PIECES[i] * P], F32, name="y_sbuf%d" % i)
-            nc.scalar.copy(out=y_sbuf[:], in_=y_psum[:])
-            return y_sbuf
-
-        turned = {}
-        products = {}
-        y_pieces = []
-        for step in range(n_pieces + 2):
-            turning = step < n_pieces
-            multiplying = 1 <= step <= n_pieces
-            if turning:
-                sum_rows = add_hops(step)
-                turned[step] = (turn_self(step), turn_neigh(step, sum_rows))
-            if multiplying:
-                y_psum = psum_y.tile([P, PIECES[step - 1] * P], F32, tag="y")
-                products[step - 1] = y_psum
-                multiply_piece(quantise_piece(step - 1, turned[step - 1]), y_psum)
-            if step >= 2:
-                y_pieces.append(measure_piece(step - 2, products[step - 2]))
+        def prepare_weights():
+            nc.vector.tensor_copy(out=w_grouped[:, 0], in_=w_raw[:, 0].rearrange("p t f -> p f t"))
+            nc.vector.tensor_scalar_mul(
+                out=w_grouped[:, 1], in0=w_raw[:, 1].rearrange("p t f -> p f t"), scalar1=0.5
+            )
+            nc.vector.quantize_mx(
+                out=w_codes[:].bitcast(FP8X4),
+                scales=w_scales[:],
+                in_=w_grouped[:].rearrange("p i f t -> p (i f t)"),
+            )
 
         gamma_f = const.tile([P, 1], F32)
         neg_gamma_f = const.tile([P, 1], F32)
         beta_f = const.tile([P, 1], F32)
+
+        def widen_affine():
+            nc.vector.tensor_copy(out=gamma_f[:], in_=gamma_bf[:])
+            nc.vector.tensor_copy(out=beta_f[:], in_=beta_bf[:])
+            nc.vector.tensor_scalar_mul(out=neg_gamma_f[:], in0=gamma_bf[:], scalar1=-1.0)
+
+        last_bank = Y_BANKS - 1
+        last_units = [i for i in range(n_units) if unit_start[i] // Y_TILES == last_bank]
+        stats = const.tile([P, last_bank + len(last_units), BN_STATS_DIM], F32)
+        y_bank = {}
+        y_home = {}
+
+        def add_hops(i):
+            n_tiles = UNITS[i]
+            h_unit = h_units[i]
+            sum_rows = grouped.tile([P, HALVES, n_tiles, FEATS // HALVES], BF16, tag="sum_rows")
+            nc.vector.tensor_tensor(
+                out=sum_rows[:].rearrange("p u g (w e) -> p g w u e", e=PAIR),
+                in0=h_unit[:, :, 1, :].rearrange("p g (w u e) -> p g w u e", u=HALVES, e=PAIR),
+                in1=h_unit[:, :, 2, :].rearrange("p g (w u e) -> p g w u e", u=HALVES, e=PAIR),
+                op=ALU.add,
+            )
+            return sum_rows
+
+        def turn_unit(i):
+            n_tiles = UNITS[i]
+            sum_rows = add_hops(i)
+            values = grouped.tile([P, SIDES, n_tiles * P * PACK], BF16, tag="values", align_bytes=64)
+            for side in range(SIDES):
+                bank = psum_turn.tile([P, HALVES * n_tiles * P], F32, tag="turn")
+                for g in range(n_tiles):
+                    for u in range(HALVES):
+                        at = (u * n_tiles + g) * P
+                        if side == 0:
+                            words = h_units[i][:, g, 0, :].bitcast(F32)[:, u::HALVES]
+                        else:
+                            words = sum_rows[:, u, g, :].bitcast(F32)
+                        nc.tensor.transpose(bank[:, at : at + P], words, ident_f32[:])
+                nc.scalar.copy(
+                    out=values[:, side, :].bitcast(F32).rearrange("p (c u) -> p c u", u=HALVES),
+                    in_=bank[:].rearrange("p (u c) -> p c u", u=HALVES),
+                )
+            return values
+
+        def quantise_unit(i, values):
+            width = UNITS[i] * P
+            words = packed.tile([P, SIDES, width], U32, tag="words", align_bytes=64)
+            scales = packed.tile([P, SIDES, width], U8, tag="scales", align_bytes=64)
+            nc.vector.quantize_mx(
+                out=words[:].rearrange("p s c -> p (s c)").bitcast(FP8X4),
+                scales=scales[:].rearrange("p s c -> p (s c)"),
+                in_=values[:].rearrange("p s c -> p (s c)"),
+            )
+            return words, scales
+
+        def multiply_unit(i, words, scales):
+            width = UNITS[i] * P
+            bank, first = divmod(unit_start[i], Y_TILES)
+            if first == 0:
+                y_bank[bank] = psum_y.tile([P, Y_TILES * P], F32, tag="y", name="y_psum")
+            for side in range(SIDES):
+                w_cols = slice(side * COLS, (side + 1) * COLS)
+                nc.tensor.matmul_mx(
+                    out=y_bank[bank][:, first * P : first * P + width],
+                    lhsT=w_codes[:, w_cols].bitcast(FP8X4),
+                    lhsT_scale=w_scales[:, w_cols],
+                    rhs=words[:, side, :].bitcast(FP8X4),
+                    rhs_scale=scales[:, side, :],
+                    start=(side == 0),
+                    stop=(side == SIDES - 1),
+                )
+
+        def measure_unit(i):
+            bank, first = divmod(unit_start[i], Y_TILES)
+            if bank == last_bank:
+                cols = slice(first * P, (first + UNITS[i]) * P)
+                nc.vector.bn_stats(
+                    out=stats[:, bank + last_units.index(i), :], in_=y_bank[bank][:, cols]
+                )
+                y_home[bank] = y_bank[bank]
+            elif first + UNITS[i] == Y_TILES:
+                nc.vector.bn_stats(out=stats[:, bank, :], in_=y_bank[bank][:])
+                y_home[bank] = y_bank[bank]
+                if bank < Y_BANKS - Y_KEPT:
+                    y_home[bank] = y_pool.tile([P, Y_TILES * P], F32, name="y_sbuf%d" % bank)
+                    nc.scalar.copy(out=y_home[bank][:], in_=y_bank[bank][:])
+
+        turned = {}
+        for step in range(n_units + MEASURE_LAG):
+            ready = step - MULTIPLY_LAG
+            multiplying = 0 <= ready < n_units
+            if multiplying:
+                words, scales = quantise_unit(ready, turned[ready])
+            if step < n_units:
+                turned[step] = turn_unit(step)
+            if multiplying:
+                multiply_unit(ready, words, scales)
+            if step >= MEASURE_LAG:
+                measure_unit(step - MEASURE_LAG)
+            if step == WEIGHTS_STEP:
+                prepare_weights()
+            if step == AFFINE_STEP:
+                widen_affine()
+
         mean_var = const.tile([P, 2], F32)
         var_eps = const.tile([P, 1], F32)
         neg_gamma_mean = const.tile([P, 1], F32)
@@ -189,9 +214,6 @@ def tile_dogtaitujuanji_pb_t_kernel(tc, h_sage, w1b, w2b, gamma, beta, out):
         nc.vector.bn_aggr(out=mean_var[:], in_=stats[:].rearrange("p i s -> p (i s)"))
         nc.vector.tensor_scalar_add(out=var_eps[:], in0=mean_var[:, 1:2], scalar1=BN_EPS)
         nc.gpsimd.tensor_tensor(out=rstd[:], in0=var_eps[:], in1=minus_half[:], op=ALU.pow)
-        nc.vector.tensor_copy(out=gamma_f[:], in_=gamma_bf[:])
-        nc.vector.tensor_copy(out=beta_f[:], in_=beta_bf[:])
-        nc.vector.tensor_scalar_mul(out=neg_gamma_f[:], in0=gamma_bf[:], scalar1=-1.0)
         nc.vector.tensor_mul(out=neg_gamma_mean[:], in0=mean_var[:, 0:1], in1=neg_gamma_f[:])
         nc.vector.tensor_mul(out=gain[:], in0=gamma_f[:], in1=rstd[:])
         nc.vector.tensor_scalar(
@@ -203,11 +225,12 @@ def tile_dogtaitujuanji_pb_t_kernel(tc, h_sage, w1b, w2b, gamma, beta, out):
             op1=ALU.add,
         )
 
-        for i, n_tiles in enumerate(PIECES):
+        for i, (start, n_tiles) in enumerate(zip(starts_of(CHUNKS), CHUNKS)):
+            bank, first = divmod(start, Y_TILES)
             sig = result.tile([P, n_tiles * P], F32, tag="sig")
             nc.scalar.activation(
                 out=sig[:],
-                in_=y_pieces[i][:],
+                in_=y_home[bank][:, first * P : (first + n_tiles) * P],
                 func=ACT.Sigmoid,
                 bias=shift[:, 0:1],
                 scale=gain[:, 0:1],
@@ -217,6 +240,4 @@ def tile_dogtaitujuanji_pb_t_kernel(tc, h_sage, w1b, w2b, gamma, beta, out):
                 nc.tensor.transpose(back[:, g, :], sig[:, g * P : (g + 1) * P], ident_f32[:])
             rows = rows_pool.tile([P, n_tiles, COLS], F32, name="rows%d" % i)
             nc.vector.tensor_copy(out=rows[:], in_=back[:])
-            nc.sync.dma_start(
-                out=out_rows[:, first_tile[i] : first_tile[i] + n_tiles, :], in_=rows[:]
-            )
+            nc.sync.dma_start(out=out_rows[:, start : start + n_tiles, :], in_=rows[:])

@@ -26,7 +26,7 @@ BN_STATS_DIM = 6
 TILES = ITEMS // P
 UNITS = (1, 1) + (2,) * 18 + (1, 1)
 MULTIPLY_LAG = 2
-MEASURE_LAG = 3
+MEASURE_LAG = 4
 WEIGHTS_STEP = 1
 AFFINE_STEP = 4
 Y_TILES = 4
@@ -56,7 +56,7 @@ def tile_dogtaitujuanji_pb_t_kernel(tc, h_sage, w1b, w2b, gamma, beta, out):
         y_pool = ctx.enter_context(tc.tile_pool(name="y_sbuf", bufs=1))
         grouped = ctx.enter_context(tc.tile_pool(name="grouped", bufs=4))
         packed = ctx.enter_context(tc.tile_pool(name="packed", bufs=4))
-        result = ctx.enter_context(tc.tile_pool(name="result", bufs=3))
+        result = ctx.enter_context(tc.tile_pool(name="result", bufs=6))
         rows_pool = ctx.enter_context(tc.tile_pool(name="rows", bufs=1))
         psum_turn = ctx.enter_context(tc.psum_pool(name="psum_turn", bufs=4))
         psum_y = ctx.enter_context(tc.psum_pool(name="psum_y", bufs=Y_KEPT))
@@ -145,7 +145,7 @@ def tile_dogtaitujuanji_pb_t_kernel(tc, h_sage, w1b, w2b, gamma, beta, out):
                 )
             return values
 
-        def quantise_unit(i, values):
+        def multiply_unit(i, values):
             width = UNITS[i] * P
             words = packed.tile([P, SIDES, width], U32, tag="words", align_bytes=64)
             scales = packed.tile([P, SIDES, width], U8, tag="scales", align_bytes=64)
@@ -154,10 +154,6 @@ def tile_dogtaitujuanji_pb_t_kernel(tc, h_sage, w1b, w2b, gamma, beta, out):
                 scales=scales[:].rearrange("p s c -> p (s c)"),
                 in_=values[:].rearrange("p s c -> p (s c)"),
             )
-            return words, scales
-
-        def multiply_unit(i, words, scales):
-            width = UNITS[i] * P
             bank, first = divmod(unit_start[i], Y_TILES)
             if first == 0:
                 y_bank[bank] = psum_y.tile([P, Y_TILES * P], F32, tag="y", name="y_psum")
@@ -190,14 +186,10 @@ def tile_dogtaitujuanji_pb_t_kernel(tc, h_sage, w1b, w2b, gamma, beta, out):
 
         turned = {}
         for step in range(n_units + MEASURE_LAG):
-            ready = step - MULTIPLY_LAG
-            multiplying = 0 <= ready < n_units
-            if multiplying:
-                words, scales = quantise_unit(ready, turned[ready])
             if step < n_units:
                 turned[step] = turn_unit(step)
-            if multiplying:
-                multiply_unit(ready, words, scales)
+            if 0 <= step - MULTIPLY_LAG < n_units:
+                multiply_unit(step - MULTIPLY_LAG, turned[step - MULTIPLY_LAG])
             if step >= MEASURE_LAG:
                 measure_unit(step - MEASURE_LAG)
             if step == WEIGHTS_STEP:

@@ -25,15 +25,17 @@ BN_STATS_DIM = 6
 
 TILES = ITEMS // P
 UNITS = (1, 1) + (2,) * 18 + (1, 1)
+LOADS = (1, 1, 2) + (4,) * 4 + (2,) * 9 + (1, 1)
 MULTIPLY_LAG = 2
 MEASURE_LAG = 4
 WEIGHTS_STEP = 1
-AFFINE_STEP = 4
+AFFINE_STEP = 8
 Y_TILES = 4
 Y_BANKS = TILES // Y_TILES
 Y_KEPT = 4
 CHUNKS = (1, 1, 2) + (4,) * 8 + (2, 1, 1)
-assert sum(UNITS) == sum(CHUNKS) == TILES
+SCALAR_COPIES = 3
+assert sum(LOADS) == sum(UNITS) == sum(CHUNKS) == TILES
 
 FLOPS = 2 * 2 * ITEMS * FEATS * COLS
 
@@ -61,11 +63,15 @@ def tile_dogtaitujuanji_pb_t_kernel(tc, h_sage, w1b, w2b, gamma, beta, out):
         psum_turn = ctx.enter_context(tc.psum_pool(name="psum_turn", bufs=4))
         psum_y = ctx.enter_context(tc.psum_pool(name="psum_y", bufs=Y_KEPT))
 
-        h_units = []
-        for i, (start, n_tiles) in enumerate(zip(unit_start, UNITS)):
-            h_unit = h_pool.tile([P, n_tiles, HOPS, FEATS], BF16, name="h_unit%d" % i)
-            nc.sync.dma_start(out=h_unit[:], in_=h_rows[:, start : start + n_tiles])
-            h_units.append(h_unit)
+        rows_of_tile = []
+        for i, (start, n_tiles) in enumerate(zip(starts_of(LOADS), LOADS)):
+            h_load = h_pool.tile([P, n_tiles, HOPS, FEATS], BF16, name="h_load%d" % i)
+            nc.sync.dma_start(out=h_load[:], in_=h_rows[:, start : start + n_tiles])
+            rows_of_tile += [(h_load, g) for g in range(n_tiles)]
+
+        def rows_of_unit(i, hop):
+            h_load, first = rows_of_tile[unit_start[i]]
+            return h_load[:, first : first + UNITS[i], hop, :]
 
         w_raw = const.tile([P, SIDES, PACK, COLS], BF16)
         nc.scalar.dma_start(out=w_raw[:, 0], in_=w2b.rearrange("(p t) f -> p t f", t=PACK))
@@ -107,6 +113,10 @@ def tile_dogtaitujuanji_pb_t_kernel(tc, h_sage, w1b, w2b, gamma, beta, out):
             nc.vector.tensor_copy(out=beta_f[:], in_=beta_bf[:])
             nc.vector.tensor_scalar_mul(out=neg_gamma_f[:], in0=gamma_bf[:], scalar1=-1.0)
 
+        def add_eps():
+            m2 = stats[:, 0, 2:3]
+            nc.vector.tensor_scalar_add(out=m2, in0=m2, scalar1=ITEMS * BN_EPS)
+
         last_bank = Y_BANKS - 1
         last_units = [i for i in range(n_units) if unit_start[i] // Y_TILES == last_bank]
         stats = const.tile([P, last_bank + len(last_units), BN_STATS_DIM], F32)
@@ -115,12 +125,11 @@ def tile_dogtaitujuanji_pb_t_kernel(tc, h_sage, w1b, w2b, gamma, beta, out):
 
         def add_hops(i):
             n_tiles = UNITS[i]
-            h_unit = h_units[i]
             sum_rows = grouped.tile([P, HALVES, n_tiles, FEATS // HALVES], BF16, tag="sum_rows")
             nc.vector.tensor_tensor(
                 out=sum_rows[:].rearrange("p u g (w e) -> p g w u e", e=PAIR),
-                in0=h_unit[:, :, 1, :].rearrange("p g (w u e) -> p g w u e", u=HALVES, e=PAIR),
-                in1=h_unit[:, :, 2, :].rearrange("p g (w u e) -> p g w u e", u=HALVES, e=PAIR),
+                in0=rows_of_unit(i, 1).rearrange("p g (w u e) -> p g w u e", u=HALVES, e=PAIR),
+                in1=rows_of_unit(i, 2).rearrange("p g (w u e) -> p g w u e", u=HALVES, e=PAIR),
                 op=ALU.add,
             )
             return sum_rows
@@ -135,7 +144,7 @@ def tile_dogtaitujuanji_pb_t_kernel(tc, h_sage, w1b, w2b, gamma, beta, out):
                     for u in range(HALVES):
                         at = (u * n_tiles + g) * P
                         if side == 0:
-                            words = h_units[i][:, g, 0, :].bitcast(F32)[:, u::HALVES]
+                            words = rows_of_unit(i, 0)[:, g, :].bitcast(F32)[:, u::HALVES]
                         else:
                             words = sum_rows[:, u, g, :].bitcast(F32)
                         nc.tensor.transpose(bank[:, at : at + P], words, ident_f32[:])
@@ -196,27 +205,26 @@ def tile_dogtaitujuanji_pb_t_kernel(tc, h_sage, w1b, w2b, gamma, beta, out):
                 prepare_weights()
             if step == AFFINE_STEP:
                 widen_affine()
+                add_eps()
 
         mean_var = const.tile([P, 2], F32)
-        var_eps = const.tile([P, 1], F32)
         neg_gamma_mean = const.tile([P, 1], F32)
         rstd = const.tile([P, 1], F32)
         gain = const.tile([P, 1], F32)
         shift = const.tile([P, 1], F32)
         nc.vector.bn_aggr(out=mean_var[:], in_=stats[:].rearrange("p i s -> p (i s)"))
-        nc.vector.tensor_scalar_add(out=var_eps[:], in0=mean_var[:, 1:2], scalar1=BN_EPS)
-        nc.gpsimd.tensor_tensor(out=rstd[:], in0=var_eps[:], in1=minus_half[:], op=ALU.pow)
+        nc.gpsimd.tensor_tensor(out=rstd[:], in0=mean_var[:, 1:2], in1=minus_half[:], op=ALU.pow)
         nc.vector.tensor_mul(out=neg_gamma_mean[:], in0=mean_var[:, 0:1], in1=neg_gamma_f[:])
-        nc.vector.tensor_mul(out=gain[:], in0=gamma_f[:], in1=rstd[:])
-        nc.vector.tensor_scalar(
+        nc.scalar.activation(out=gain[:], in_=rstd[:], func=ACT.Copy, scale=gamma_f[:, 0:1])
+        nc.scalar.activation(
             out=shift[:],
-            in0=neg_gamma_mean[:],
-            scalar1=rstd[:, 0:1],
-            scalar2=beta_f[:, 0:1],
-            op0=ALU.mult,
-            op1=ALU.add,
+            in_=rstd[:],
+            func=ACT.Identity,
+            scale=neg_gamma_mean[:, 0:1],
+            bias=beta_f[:, 0:1],
         )
 
+        late = []
         for i, (start, n_tiles) in enumerate(zip(starts_of(CHUNKS), CHUNKS)):
             bank, first = divmod(start, Y_TILES)
             sig = result.tile([P, n_tiles * P], F32, tag="sig")
@@ -227,9 +235,19 @@ def tile_dogtaitujuanji_pb_t_kernel(tc, h_sage, w1b, w2b, gamma, beta, out):
                 bias=shift[:, 0:1],
                 scale=gain[:, 0:1],
             )
-            back = psum_turn.tile([P, n_tiles, COLS], F32, tag="turn")
+            if i < len(CHUNKS) - SCALAR_COPIES:
+                back = psum_turn.tile([P, n_tiles, COLS], F32, tag="turn")
+            else:
+                back = psum_y.tile([P, n_tiles, COLS], F32, tag="y", name="back_late")
             for g in range(n_tiles):
                 nc.tensor.transpose(back[:, g, :], sig[:, g * P : (g + 1) * P], ident_f32[:])
             rows = rows_pool.tile([P, n_tiles, COLS], F32, name="rows%d" % i)
-            nc.vector.tensor_copy(out=rows[:], in_=back[:])
-            nc.sync.dma_start(out=out_rows[:, start : start + n_tiles, :], in_=rows[:])
+            store = (out_rows[:, start : start + n_tiles, :], rows, back)
+            if i < len(CHUNKS) - SCALAR_COPIES:
+                nc.vector.tensor_copy(out=rows[:], in_=back[:])
+                nc.sync.dma_start(out=store[0], in_=rows[:])
+            else:
+                late.append(store)
+        for rows_out, rows, back in late:
+            nc.scalar.copy(out=rows[:], in_=back[:])
+            nc.sync.dma_start(out=rows_out, in_=rows[:])

@@ -21,6 +21,7 @@ HOPS = 3
 FEATS = 512
 COLS = 128
 BN_EPS = 1e-5
+DMA_ALIGN = 512
 BN_STATS_DIM = 6
 
 TILES = ITEMS // P
@@ -65,7 +66,9 @@ def tile_dogtaitujuanji_pb_t_kernel(tc, h_sage, w1b, w2b, gamma, beta, out):
 
         rows_of_tile = []
         for i, (start, n_tiles) in enumerate(zip(starts_of(LOADS), LOADS)):
-            h_load = h_pool.tile([P, n_tiles, HOPS, FEATS], BF16, name="h_load%d" % i)
+            h_load = h_pool.tile(
+                [P, n_tiles, HOPS, FEATS], BF16, name="h_load%d" % i, align_bytes=DMA_ALIGN
+            )
             nc.sync.dma_start(out=h_load[:], in_=h_rows[:, start : start + n_tiles])
             rows_of_tile += [(h_load, g) for g in range(n_tiles)]
 
@@ -73,7 +76,7 @@ def tile_dogtaitujuanji_pb_t_kernel(tc, h_sage, w1b, w2b, gamma, beta, out):
             h_load, first = rows_of_tile[unit_start[i]]
             return h_load[:, first : first + UNITS[i], hop, :]
 
-        w_raw = const.tile([P, SIDES, PACK, COLS], BF16)
+        w_raw = const.tile([P, SIDES, PACK, COLS], BF16, align_bytes=DMA_ALIGN)
         nc.scalar.dma_start(out=w_raw[:, 0], in_=w2b.rearrange("(p t) f -> p t f", t=PACK))
         nc.scalar.dma_start(out=w_raw[:, 1], in_=w1b.rearrange("(p t) f -> p t f", t=PACK))
         gamma_bf = const.tile([P, 1], BF16)
@@ -241,7 +244,7 @@ def tile_dogtaitujuanji_pb_t_kernel(tc, h_sage, w1b, w2b, gamma, beta, out):
                 back = psum_y.tile([P, n_tiles, COLS], F32, tag="y", name="back_late")
             for g in range(n_tiles):
                 nc.tensor.transpose(back[:, g, :], sig[:, g * P : (g + 1) * P], ident_f32[:])
-            rows = rows_pool.tile([P, n_tiles, COLS], F32, name="rows%d" % i)
+            rows = rows_pool.tile([P, n_tiles, COLS], F32, name="rows%d" % i, align_bytes=DMA_ALIGN)
             store = (out_rows[:, start : start + n_tiles, :], rows, back)
             if i < len(CHUNKS) - SCALAR_COPIES:
                 nc.vector.tensor_copy(out=rows[:], in_=back[:])

@@ -30,7 +30,8 @@ LOADS = (1, 1, 2) + (4,) * 4 + (2,) * 9 + (1, 1)
 MULTIPLY_LAG = 2
 MEASURE_LAG = 4
 WEIGHTS_STEP = 1
-AFFINE_STEP = 8
+AFFINE_STEP = 2
+EPS_STEP = 8
 Y_TILES = 4
 Y_BANKS = TILES // Y_TILES
 Y_KEPT = 4
@@ -79,10 +80,10 @@ def tile_dogtaitujuanji_pb_t_kernel(tc, h_sage, w1b, w2b, gamma, beta, out):
         w_raw = const.tile([P, SIDES, PACK, COLS], BF16, align_bytes=DMA_ALIGN)
         nc.scalar.dma_start(out=w_raw[:, 0], in_=w2b.rearrange("(p t) f -> p t f", t=PACK))
         nc.scalar.dma_start(out=w_raw[:, 1], in_=w1b.rearrange("(p t) f -> p t f", t=PACK))
-        gamma_bf = const.tile([P, 1], BF16)
-        beta_bf = const.tile([P, 1], BF16)
-        nc.scalar.dma_start(out=gamma_bf[:], in_=gamma.rearrange("(f o) -> f o", o=1))
-        nc.scalar.dma_start(out=beta_bf[:], in_=beta.rearrange("(f o) -> f o", o=1))
+        affine_rows = const.tile([P, P], BF16)
+        nc.vector.memset(affine_rows[:], 0.0)
+        nc.scalar.dma_start(out=affine_rows[0:1, :], in_=gamma.rearrange("(o f) -> o f", o=1))
+        nc.scalar.dma_start(out=affine_rows[1:2, :], in_=beta.rearrange("(o f) -> o f", o=1))
 
         ident_f32 = const.tile([P, P], F32)
         make_identity(nc, ident_f32[:])
@@ -107,14 +108,18 @@ def tile_dogtaitujuanji_pb_t_kernel(tc, h_sage, w1b, w2b, gamma, beta, out):
                 in_=w_grouped[:].rearrange("p i f t -> p (i f t)"),
             )
 
-        gamma_f = const.tile([P, 1], F32)
+        ident_bf16 = const.tile([P, P], BF16)
+        affine_f = const.tile([P, 2], F32)
+        gamma_f = affine_f[:, 0:1]
+        beta_f = affine_f[:, 1:2]
         neg_gamma_f = const.tile([P, 1], F32)
-        beta_f = const.tile([P, 1], F32)
 
-        def widen_affine():
-            nc.vector.tensor_copy(out=gamma_f[:], in_=gamma_bf[:])
-            nc.vector.tensor_copy(out=beta_f[:], in_=beta_bf[:])
-            nc.vector.tensor_scalar_mul(out=neg_gamma_f[:], in0=gamma_bf[:], scalar1=-1.0)
+        def turn_affine():
+            nc.vector.tensor_copy(out=ident_bf16[:], in_=ident_f32[:])
+            bank = psum_turn.tile([P, P], BF16, tag="turn")
+            nc.tensor.transpose(bank[:], affine_rows[:], ident_bf16[:])
+            nc.vector.tensor_copy(out=affine_f[:], in_=bank[:, 0:2])
+            nc.vector.tensor_scalar_mul(out=neg_gamma_f[:], in0=gamma_f, scalar1=-1.0)
 
         def add_eps():
             m2 = stats[:, 0, 2:3]
@@ -207,7 +212,8 @@ def tile_dogtaitujuanji_pb_t_kernel(tc, h_sage, w1b, w2b, gamma, beta, out):
             if step == WEIGHTS_STEP:
                 prepare_weights()
             if step == AFFINE_STEP:
-                widen_affine()
+                turn_affine()
+            if step == EPS_STEP:
                 add_eps()
 
         mean_var = const.tile([P, 2], F32)
@@ -218,13 +224,13 @@ def tile_dogtaitujuanji_pb_t_kernel(tc, h_sage, w1b, w2b, gamma, beta, out):
         nc.vector.bn_aggr(out=mean_var[:], in_=stats[:].rearrange("p i s -> p (i s)"))
         nc.gpsimd.tensor_tensor(out=rstd[:], in0=mean_var[:, 1:2], in1=minus_half[:], op=ALU.pow)
         nc.vector.tensor_mul(out=neg_gamma_mean[:], in0=mean_var[:, 0:1], in1=neg_gamma_f[:])
-        nc.scalar.activation(out=gain[:], in_=rstd[:], func=ACT.Copy, scale=gamma_f[:, 0:1])
+        nc.scalar.activation(out=gain[:], in_=rstd[:], func=ACT.Copy, scale=gamma_f)
         nc.scalar.activation(
             out=shift[:],
             in_=rstd[:],
             func=ACT.Identity,
             scale=neg_gamma_mean[:, 0:1],
-            bias=beta_f[:, 0:1],
+            bias=beta_f,
         )
 
         late = []

@@ -22,7 +22,8 @@ FEATS = 512
 COLS = 128
 BN_EPS = 1e-5
 DMA_ALIGN = 512
-BN_STATS_DIM = 6
+BN_TRIPLE = 3
+BN_STATS_DIM = 2 * BN_TRIPLE
 
 TILES = ITEMS // P
 UNITS = (1, 1) + (2,) * 18 + (1, 1)
@@ -31,12 +32,14 @@ MULTIPLY_LAG = 2
 MEASURE_LAG = 4
 WEIGHTS_STEP = 1
 AFFINE_STEP = 2
-EPS_STEP = 8
+AFFINE_COPY_STEP = 5
+EARLY_BANKS = 6
+JOIN_STEP = 17
 Y_TILES = 4
 Y_BANKS = TILES // Y_TILES
 Y_KEPT = 4
-CHUNKS = (1, 1, 2) + (4,) * 8 + (2, 1, 1)
-SCALAR_COPIES = 3
+CHUNKS = (1, 1, 2) + (4,) * 8 + (2, 2)
+SCALAR_COPIES = 2
 assert sum(LOADS) == sum(UNITS) == sum(CHUNKS) == TILES
 
 FLOPS = 2 * 2 * ITEMS * FEATS * COLS
@@ -87,6 +90,8 @@ def tile_dogtaitujuanji_pb_t_kernel(tc, h_sage, w1b, w2b, gamma, beta, out):
 
         ident_f32 = const.tile([P, P], F32)
         make_identity(nc, ident_f32[:])
+        ident_bf16 = const.tile([P, P], BF16)
+        nc.gpsimd.tensor_copy(out=ident_bf16[:], in_=ident_f32[:])
         minus_half = const.tile([P, 1], F32)
         nc.vector.memset(minus_half[:], -0.5)
         warm = const.tile([P, 1], F32)
@@ -108,26 +113,44 @@ def tile_dogtaitujuanji_pb_t_kernel(tc, h_sage, w1b, w2b, gamma, beta, out):
                 in_=w_grouped[:].rearrange("p i f t -> p (i f t)"),
             )
 
-        ident_bf16 = const.tile([P, P], BF16)
         affine_f = const.tile([P, 2], F32)
         gamma_f = affine_f[:, 0:1]
         beta_f = affine_f[:, 1:2]
         neg_gamma_f = const.tile([P, 1], F32)
 
         def turn_affine():
-            nc.vector.tensor_copy(out=ident_bf16[:], in_=ident_f32[:])
-            bank = psum_turn.tile([P, P], BF16, tag="turn")
+            bank = psum_y.tile([P, P], BF16, tag="y", name="affine_bank")
             nc.tensor.transpose(bank[:], affine_rows[:], ident_bf16[:])
+            return bank
+
+        def copy_affine(bank):
             nc.vector.tensor_copy(out=affine_f[:], in_=bank[:, 0:2])
             nc.vector.tensor_scalar_mul(out=neg_gamma_f[:], in0=gamma_f, scalar1=-1.0)
 
-        def add_eps():
-            m2 = stats[:, 0, 2:3]
-            nc.vector.tensor_scalar_add(out=m2, in0=m2, scalar1=ITEMS * BN_EPS)
+        def join_early_stats():
+            nc.vector.bn_aggr(out=late_stats[:, 1:3], in_=stats[:].rearrange("p i s -> p (i s)"))
+            m2 = late_stats[:, 2:3]
+            nc.vector.tensor_scalar(
+                out=m2,
+                in0=m2,
+                scalar1=float(EARLY_BANKS * Y_TILES * P),
+                scalar2=ITEMS * BN_EPS,
+                op0=ALU.mult,
+                op1=ALU.add,
+            )
 
         last_bank = Y_BANKS - 1
         last_units = [i for i in range(n_units) if unit_start[i] // Y_TILES == last_bank]
-        stats = const.tile([P, last_bank + len(last_units), BN_STATS_DIM], F32)
+        stats = const.tile([P, EARLY_BANKS, BN_STATS_DIM], F32)
+        late_stats = const.tile(
+            [P, BN_TRIPLE + (last_bank - EARLY_BANKS + len(last_units)) * BN_STATS_DIM], F32
+        )
+        nc.vector.memset(late_stats[:, 0:1], float(EARLY_BANKS * Y_TILES * P))
+
+        def late_stats_of(k):
+            at = BN_TRIPLE + k * BN_STATS_DIM
+            return late_stats[:, at : at + BN_STATS_DIM]
+
         y_bank = {}
         y_home = {}
 
@@ -191,11 +214,14 @@ def tile_dogtaitujuanji_pb_t_kernel(tc, h_sage, w1b, w2b, gamma, beta, out):
             if bank == last_bank:
                 cols = slice(first * P, (first + UNITS[i]) * P)
                 nc.vector.bn_stats(
-                    out=stats[:, bank + last_units.index(i), :], in_=y_bank[bank][:, cols]
+                    out=late_stats_of(last_bank - EARLY_BANKS + last_units.index(i)),
+                    in_=y_bank[bank][:, cols],
                 )
                 y_home[bank] = y_bank[bank]
             elif first + UNITS[i] == Y_TILES:
-                nc.vector.bn_stats(out=stats[:, bank, :], in_=y_bank[bank][:])
+                early = bank < EARLY_BANKS
+                bank_stats = stats[:, bank, :] if early else late_stats_of(bank - EARLY_BANKS)
+                nc.vector.bn_stats(out=bank_stats, in_=y_bank[bank][:])
                 y_home[bank] = y_bank[bank]
                 if bank < Y_BANKS - Y_KEPT:
                     y_home[bank] = y_pool.tile([P, Y_TILES * P], F32, name="y_sbuf%d" % bank)
@@ -212,16 +238,18 @@ def tile_dogtaitujuanji_pb_t_kernel(tc, h_sage, w1b, w2b, gamma, beta, out):
             if step == WEIGHTS_STEP:
                 prepare_weights()
             if step == AFFINE_STEP:
-                turn_affine()
-            if step == EPS_STEP:
-                add_eps()
+                affine_bank = turn_affine()
+            if step == AFFINE_COPY_STEP:
+                copy_affine(affine_bank)
+            if step == JOIN_STEP:
+                join_early_stats()
 
         mean_var = const.tile([P, 2], F32)
         neg_gamma_mean = const.tile([P, 1], F32)
         rstd = const.tile([P, 1], F32)
         gain = const.tile([P, 1], F32)
         shift = const.tile([P, 1], F32)
-        nc.vector.bn_aggr(out=mean_var[:], in_=stats[:].rearrange("p i s -> p (i s)"))
+        nc.vector.bn_aggr(out=mean_var[:], in_=late_stats[:])
         nc.gpsimd.tensor_tensor(out=rstd[:], in0=mean_var[:, 1:2], in1=minus_half[:], op=ALU.pow)
         nc.vector.tensor_mul(out=neg_gamma_mean[:], in0=mean_var[:, 0:1], in1=neg_gamma_f[:])
         nc.scalar.activation(out=gain[:], in_=rstd[:], func=ACT.Copy, scale=gamma_f)

@@ -30,6 +30,7 @@ UNITS = (1, 1) + (2,) * 18 + (1, 1)
 LOADS = (1, 1, 2) + (4,) * 4 + (2,) * 9 + (1, 1)
 MULTIPLY_LAG = 2
 MEASURE_LAG = 4
+LATE_UNITS = 4
 WEIGHTS_STEP = 1
 AFFINE_STEP = 2
 AFFINE_COPY_STEP = 5
@@ -189,11 +190,13 @@ def tile_dogtaitujuanji_pb_t_kernel(tc, h_sage, w1b, w2b, gamma, beta, out):
             width = UNITS[i] * P
             words = packed.tile([P, SIDES, width], U32, tag="words", align_bytes=64)
             scales = packed.tile([P, SIDES, width], U8, tag="scales", align_bytes=64)
-            nc.vector.quantize_mx(
-                out=words[:].rearrange("p s c -> p (s c)").bitcast(FP8X4),
-                scales=scales[:].rearrange("p s c -> p (s c)"),
-                in_=values[:].rearrange("p s c -> p (s c)"),
-            )
+            late = i >= n_units - LATE_UNITS
+            for sides in [slice(0, 1), slice(1, 2)] if late else [slice(0, SIDES)]:
+                nc.vector.quantize_mx(
+                    out=words[:, sides, :].rearrange("p s c -> p (s c)").bitcast(FP8X4),
+                    scales=scales[:, sides, :].rearrange("p s c -> p (s c)"),
+                    in_=values[:, sides, :].rearrange("p s c -> p (s c)"),
+                )
             bank, first = divmod(unit_start[i], Y_TILES)
             if first == 0:
                 y_bank[bank] = psum_y.tile([P, Y_TILES * P], F32, tag="y", name="y_psum")

from contextlib import ExitStack

import concourse.mybir as mybir
from concourse.masks import make_identity

BF16 = mybir.dt.bfloat16
F32 = mybir.dt.float32
U32 = mybir.dt.uint32
U8 = mybir.dt.uint8
FP8X4 = mybir.dt.float8_e4m3fn_x4
ALU = mybir.AluOpType
ACT = mybir.ActivationFunctionType

P = 128
PACK = 4
HALVES = 2
PAIR = 2
SIDES = 2
ITEMS = 5120
HOPS = 3
FEATS = 512
COLS = 128
BN_EPS = 1e-5
DMA_ALIGN = 512
BN_TRIPLE = 3
BN_STATS_DIM = 2 * BN_TRIPLE

TILES = ITEMS // P
UNITS = (1, 1) + (2,) * 18 + (1, 1)
LOADS = (1, 1, 2) + (4,) * 4 + (2,) * 9 + (1, 1)
MULTIPLY_LAG = 2
MEASURE_LAG = 4
LATE_UNITS = 4
WEIGHTS_STEP = 1
AFFINE_STEP = 2
AFFINE_COPY_STEP = 5
EARLY_BANKS = 6
JOIN_STEP = 17
Y_TILES = 4
Y_BANKS = TILES // Y_TILES
Y_KEPT = 4
CHUNKS = (1, 1, 2) + (4,) * 8 + (2, 2)
SCALAR_COPIES = 2
assert sum(LOADS) == sum(UNITS) == sum(CHUNKS) == TILES

FLOPS = 2 * 2 * ITEMS * FEATS * COLS


def starts_of(sizes):
    return [sum(sizes[:i]) for i in range(len(sizes))]


def tile_dogtaitujuanji_pb_t_kernel(tc, h_sage, w1b, w2b, gamma, beta, out):
    nc = tc.nc
    h_rows = h_sage.rearrange("(p j) q k -> p j q k", j=TILES)
    out_rows = out.rearrange("(p j) f -> p j f", j=TILES)
    n_units = len(UNITS)
    unit_start = starts_of(UNITS)

    with ExitStack() as ctx:
        ctx.enter_context(tc.manual_schedule())
        const = ctx.enter_context(tc.tile_pool(name="const", bufs=1))
        h_pool = ctx.enter_context(tc.tile_pool(name="h", bufs=1))
        y_pool = ctx.enter_context(tc.tile_pool(name="y_sbuf", bufs=1))
        grouped = ctx.enter_context(tc.tile_pool(name="grouped", bufs=4))
        packed = ctx.enter_context(tc.tile_pool(name="packed", bufs=4))
        result = ctx.enter_context(tc.tile_pool(name="result", bufs=6))
        rows_pool = ctx.enter_context(tc.tile_pool(name="rows", bufs=1))
        psum_turn = ctx.enter_context(tc.psum_pool(name="psum_turn", bufs=4))
        psum_y = ctx.enter_context(tc.psum_pool(name="psum_y", bufs=Y_KEPT))

        rows_of_tile = []
        for i, (start, n_tiles) in enumerate(zip(starts_of(LOADS), LOADS)):
            h_load = h_pool.tile(
                [P, n_tiles, HOPS, FEATS], BF16, name="h_load%d" % i, align_bytes=DMA_ALIGN
            )
            nc.sync.dma_start(out=h_load[:], in_=h_rows[:, start : start + n_tiles])
            rows_of_tile += [(h_load, g) for g in range(n_tiles)]

        def rows_of_unit(i, hop):
            h_load, first = rows_of_tile[unit_start[i]]
            return h_load[:, first : first + UNITS[i], hop, :]

        w_raw = const.tile([P, SIDES, PACK, COLS], BF16, align_bytes=DMA_ALIGN)
        nc.scalar.dma_start(out=w_raw[:, 0], in_=w2b.rearrange("(p t) f -> p t f", t=PACK))
        nc.scalar.dma_start(out=w_raw[:, 1], in_=w1b.rearrange("(p t) f -> p t f", t=PACK))
        affine_rows = const.tile([P, P], BF16)
        nc.vector.memset(affine_rows[:], 0.0)
        nc.scalar.dma_start(out=affine_rows[0:1, :], in_=gamma.rearrange("(o f) -> o f", o=1))
        nc.scalar.dma_start(out=affine_rows[1:2, :], in_=beta.rearrange("(o f) -> o f", o=1))

        ident_f32 = const.tile([P, P], F32)
        make_identity(nc, ident_f32[:])
        ident_bf16 = const.tile([P, P], BF16)
        nc.gpsimd.tensor_copy(out=ident_bf16[:], in_=ident_f32[:])
        minus_half = const.tile([P, 1], F32)
        nc.vector.memset(minus_half[:], -0.5)
        warm = const.tile([P, 1], F32)
        nc.vector.memset(warm[:], 0.0)
        nc.scalar.activation(out=warm[:], in_=warm[:], func=ACT.Sigmoid)

        w_grouped = const.tile([P, SIDES, COLS, PACK], BF16, align_bytes=64)
        w_codes = const.tile([P, SIDES * COLS], U32, align_bytes=64)
        w_scales = const.tile([P, SIDES * COLS], U8, align_bytes=64)

        def prepare_weights():
            nc.vector.tensor_copy(out=w_grouped[:, 0], in_=w_raw[:, 0].rearrange("p t f -> p f t"))
            nc.vector.tensor_scalar_mul(
                out=w_grouped[:, 1], in0=w_raw[:, 1].rearrange("p t f -> p f t"), scalar1=0.5
            )
            nc.vector.quantize_mx(
                out=w_codes[:].bitcast(FP8X4),
                scales=w_scales[:],
                in_=w_grouped[:].rearrange("p i f t -> p (i f t)"),
            )

        affine_f = const.tile([P, 2], F32)
        gamma_f = affine_f[:, 0:1]
        beta_f = affine_f[:, 1:2]
        neg_gamma_f = const.tile([P, 1], F32)

        def turn_affine():
            bank = psum_y.tile([P, P], BF16, tag="y", name="affine_bank")
            nc.tensor.transpose(bank[:], affine_rows[:], ident_bf16[:])
            return bank

        def copy_affine(bank):
            nc.vector.tensor_copy(out=affine_f[:], in_=bank[:, 0:2])
            nc.vector.tensor_scalar_mul(out=neg_gamma_f[:], in0=gamma_f, scalar1=-1.0)

        def join_early_stats():
            nc.vector.bn_aggr(out=late_stats[:, 1:3], in_=stats[:].rearrange("p i s -> p (i s)"))
            m2 = late_stats[:, 2:3]
            nc.vector.tensor_scalar(
                out=m2,
                in0=m2,
                scalar1=float(EARLY_BANKS * Y_TILES * P),
                scalar2=ITEMS * BN_EPS,
                op0=ALU.mult,
                op1=ALU.add,
            )

        last_bank = Y_BANKS - 1
        last_units = [i for i in range(n_units) if unit_start[i] // Y_TILES == last_bank]
        stats = const.tile([P, EARLY_BANKS, BN_STATS_DIM], F32)
        late_stats = const.tile(
            [P, BN_TRIPLE + (last_bank - EARLY_BANKS + len(last_units)) * BN_STATS_DIM], F32
        )
        nc.vector.memset(late_stats[:, 0:1], float(EARLY_BANKS * Y_TILES * P))

        def late_stats_of(k):
            at = BN_TRIPLE + k * BN_STATS_DIM
            return late_stats[:, at : at + BN_STATS_DIM]

        y_bank = {}
        y_home = {}

        def add_hops(i):
            n_tiles = UNITS[i]
            sum_rows = grouped.tile([P, HALVES, n_tiles, FEATS // HALVES], BF16, tag="sum_rows")
            nc.vector.tensor_tensor(
                out=sum_rows[:].rearrange("p u g (w e) -> p g w u e", e=PAIR),
                in0=rows_of_unit(i, 1).rearrange("p g (w u e) -> p g w u e", u=HALVES, e=PAIR),
                in1=rows_of_unit(i, 2).rearrange("p g (w u e) -> p g w u e", u=HALVES, e=PAIR),
                op=ALU.add,
            )
            return sum_rows

        def turn_unit(i):
            n_tiles = UNITS[i]
            sum_rows = add_hops(i)
            values = grouped.tile([P, SIDES, n_tiles * P * PACK], BF16, tag="values", align_bytes=64)
            for side in range(SIDES):
                bank = psum_turn.tile([P, HALVES * n_tiles * P], F32, tag="turn")
                for g in range(n_tiles):
                    for u in range(HALVES):
                        at = (u * n_tiles + g) * P
                        if side == 0:
                            words = rows_of_unit(i, 0)[:, g, :].bitcast(F32)[:, u::HALVES]
                        else:
                            words = sum_rows[:, u, g, :].bitcast(F32)
                        nc.tensor.transpose(bank[:, at : at + P], words, ident_f32[:])
                nc.scalar.copy(
                    out=values[:, side, :].bitcast(F32).rearrange("p (c u) -> p c u", u=HALVES),
                    in_=bank[:].rearrange("p (u c) -> p c u", u=HALVES),
                )
            return values

        def multiply_unit(i, values):
            width = UNITS[i] * P
            words = packed.tile([P, SIDES, width], U32, tag="words", align_bytes=64)
            scales = packed.tile([P, SIDES, width], U8, tag="scales", align_bytes=64)
            late = i >= n_units - LATE_UNITS
            for sides in [slice(0, 1), slice(1, 2)] if late else [slice(0, SIDES)]:
                nc.vector.quantize_mx(
                    out=words[:, sides, :].rearrange("p s c -> p (s c)").bitcast(FP8X4),
                    scales=scales[:, sides, :].rearrange("p s c -> p (s c)"),
                    in_=values[:, sides, :].rearrange("p s c -> p (s c)"),
                )
            bank, first = divmod(unit_start[i], Y_TILES)
            if first == 0:
                y_bank[bank] = psum_y.tile([P, Y_TILES * P], F32, tag="y", name="y_psum")
            for side in range(SIDES):
                w_cols = slice(side * COLS, (side + 1) * COLS)
                nc.tensor.matmul_mx(
                    out=y_bank[bank][:, first * P : first * P + width],
                    lhsT=w_codes[:, w_cols].bitcast(FP8X4),
                    lhsT_scale=w_scales[:, w_cols],
                    rhs=words[:, side, :].bitcast(FP8X4),
                    rhs_scale=scales[:, side, :],
                    start=(side == 0),
                    stop=(side == SIDES - 1),
                )

        def measure_unit(i):
            bank, first = divmod(unit_start[i], Y_TILES)
            if bank == last_bank:
                cols = slice(first * P, (first + UNITS[i]) * P)
                nc.vector.bn_stats(
                    out=late_stats_of(last_bank - EARLY_BANKS + last_units.index(i)),
                    in_=y_bank[bank][:, cols],
                )
                y_home[bank] = y_bank[bank]
            elif first + UNITS[i] == Y_TILES:
                early = bank < EARLY_BANKS
                bank_stats = stats[:, bank, :] if early else late_stats_of(bank - EARLY_BANKS)
                nc.vector.bn_stats(out=bank_stats, in_=y_bank[bank][:])
                y_home[bank] = y_bank[bank]
                if bank < Y_BANKS - Y_KEPT:
                    y_home[bank] = y_pool.tile([P, Y_TILES * P], F32, name="y_sbuf%d" % bank)
                    nc.scalar.copy(out=y_home[bank][:], in_=y_bank[bank][:])

        turned = {}
        for step in range(n_units + MEASURE_LAG):
            if step < n_units:
                turned[step] = turn_unit(step)
            if 0 <= step - MULTIPLY_LAG < n_units:
                multiply_unit(step - MULTIPLY_LAG, turned[step - MULTIPLY_LAG])
            if step >= MEASURE_LAG:
                measure_unit(step - MEASURE_LAG)
            if step == WEIGHTS_STEP:
                prepare_weights()
            if step == AFFINE_STEP:
                affine_bank = turn_affine()
            if step == AFFINE_COPY_STEP:
                copy_affine(affine_bank)
            if step == JOIN_STEP:
                join_early_stats()

        mean_var = const.tile([P, 2], F32)
        neg_gamma_mean = const.tile([P, 1], F32)
        rstd = const.tile([P, 1], F32)
        gain = const.tile([P, 1], F32)
        shift = const.tile([P, 1], F32)
        nc.vector.bn_aggr(out=mean_var[:], in_=late_stats[:])
        nc.gpsimd.tensor_tensor(out=rstd[:], in0=mean_var[:, 1:2], in1=minus_half[:], op=ALU.pow)
        nc.vector.tensor_mul(out=neg_gamma_mean[:], in0=mean_var[:, 0:1], in1=neg_gamma_f[:])
        nc.scalar.activation(out=gain[:], in_=rstd[:], func=ACT.Copy, scale=gamma_f)
        nc.scalar.activation(
            out=shift[:],
            in_=rstd[:],
            func=ACT.Identity,
            scale=neg_gamma_mean[:, 0:1],
            bias=beta_f,
        )

        late = []
        for i, (start, n_tiles) in enumerate(zip(starts_of(CHUNKS), CHUNKS)):
            bank, first = divmod(start, Y_TILES)
            sig = result.tile([P, n_tiles * P], F32, tag="sig")
            nc.scalar.activation(
                out=sig[:],
                in_=y_home[bank][:, first * P : (first + n_tiles) * P],
                func=ACT.Sigmoid,
                bias=shift[:, 0:1],
                scale=gain[:, 0:1],
            )
            if i < len(CHUNKS) - SCALAR_COPIES:
                back = psum_turn.tile([P, n_tiles, COLS], F32, tag="turn")
            else:
                back = psum_y.tile([P, n_tiles, COLS], F32, tag="y", name="back_late")
            for g in range(n_tiles):
                nc.tensor.transpose(back[:, g, :], sig[:, g * P : (g + 1) * P], ident_f32[:])
            rows = rows_pool.tile([P, n_tiles, COLS], F32, name="rows%d" % i, align_bytes=DMA_ALIGN)
            store = (out_rows[:, start : start + n_tiles, :], rows, back)
            if i < len(CHUNKS) - SCALAR_COPIES:
                nc.vector.tensor_copy(out=rows[:], in_=back[:])
                nc.sync.dma_start(out=store[0], in_=rows[:])
            else:
                late.append(store)
        for rows_out, rows, back in late:
            nc.scalar.copy(out=rows[:], in_=back[:])
            nc.sync.dma_start(out=rows_out, in_=rows[:])
